import numpy as np
import ml_dtypes


def mxq(x, axis, fmt="e4m3"):
    dtype, down = {"e4m3": (ml_dtypes.float8_e4m3fn, 7), "e5m2": (ml_dtypes.float8_e5m2, 14)}[fmt]
    v = np.moveaxis(np.asarray(x, np.float32).astype(ml_dtypes.bfloat16).astype(np.float64), axis, -1)
    blocks = v.reshape(v.shape[:-1] + (-1, 32))
    amax = np.abs(blocks).max(-1, keepdims=True)
    byte = np.maximum(np.where(amax > 0, np.frexp(amax)[1] - 1 + 127, 0) - down, 1)
    scale = np.exp2(byte - 127.0)
    codes = (blocks / scale).astype(np.float32).astype(dtype).astype(np.float64)
    return np.moveaxis((codes * scale).reshape(v.shape), -1, axis)


WIDE = False


def mx_kscale(k):
    if not WIDE:
        return np.ones(k)
    levels = np.array([10, -10, 5, -5, 0])
    a = np.random.permutation(np.resize(levels, k // 512 * 4)).reshape(k // 512, 4)
    idx = np.arange(k)
    return np.exp2(a[idx // 512, idx % 128 // 32])


BF16 = ml_dtypes.bfloat16


def bf(x):
    return np.asarray(x, np.float32).astype(BF16)


def f64(x):
    return np.asarray(x).astype(np.float64)


B, N, HID, H, D = 2, 128, 2048, 16, 128


def apply_rope(t, rope):
    freqs = rope[:, 0, :]
    cos = np.repeat(freqs[:, 0::2], 2, axis=-1)[None, None]
    sin = np.repeat(freqs[:, 1::2], 2, axis=-1)[None, None]
    tr = t.reshape(*t.shape[:-1], -1, 2)
    t_real, t_imag = tr[..., 0], tr[..., 1]
    t_rot = np.stack([-t_imag, t_real], axis=-1).reshape(t.shape)
    return t * cos + t_rot * sin


def setup_inputs():
    s = mx_kscale(HID)
    return {"x": bf(np.random.standard_normal((B, N, HID)) * s),
            "rope": bf(np.random.uniform(size=(N, 1, D))),
            "qkv_w": bf(np.random.standard_normal((HID, 3 * H * D)) * 1.5 / np.sqrt(HID) / s[:, None])}


def reference(x, rope, qkv_w):
    r = f64(rope)
    qkv = (mxq(f64(x), 2, "e4m3") @ mxq(f64(qkv_w), 0, "e4m3")).reshape(B, N, 3, H, D)
    q = np.transpose(qkv[:, :, 0], (0, 2, 1, 3))
    k = np.transpose(qkv[:, :, 1], (0, 2, 1, 3))
    v = np.transpose(qkv[:, :, 2], (0, 2, 1, 3))
    return apply_rope(q, r), apply_rope(k, r), v

@@ -1,0 +1,225 @@
+from contextlib import ExitStack
+
+import concourse.mybir as mybir
+from concourse.masks import make_identity
+
+F32 = mybir.dt.float32
+BF16 = mybir.dt.bfloat16
+U32 = mybir.dt.uint32
+U8 = mybir.dt.uint8
+FP8X4 = mybir.dt.float8_e4m3fn_x4
+MULT = mybir.AluOpType.mult
+ADD = mybir.AluOpType.add
+
+FLOPS = 2 * 256 * 2048 * 6144
+
+P = 128
+NB = 6
+GB = 6
+CB = 16
+TB = 3
+SB = 4
+LQ = 1
+LE = 1
+X_AFTER = 1
+ENG = "VSSVVSVSVSVSVSVS" + "SSSSSSSSSVSVSVSS" + "SSSSSSSSVSSVSVSV"
+HYBRID = (False, False, True)
+ADD_ENGINE = "V"
+MANUAL = True
+
+
+def sub_block_order():
+    order = []
+    for g in range(3):
+        if HYBRID[g]:
+            for c in range(2):
+                for nb in range(4):
+                    order.append((g, c, nb))
+            for nb in range(4):
+                for c in range(2, 4):
+                    order.append((g, c, nb))
+        else:
+            for c in range(4):
+                for nb in range(4):
+                    order.append((g, c, nb))
+    return order
+
+
+def tile_attention_pa_kernel(tc, x, rope, qkv_w, out_0, out_1, out_2):
+    nc = tc.nc
+    outs = (out_0, out_1, out_2)
+    order = sub_block_order()
+    n_sub = len(order)
+    last_of = {}
+    for s, (g, c, nb) in enumerate(order):
+        last_of[(g, nb)] = s
+    users = {}
+    chunk_seq = []
+    for s, (g, c, nb) in enumerate(order):
+        ch = 4 * g + c
+        if ch not in users:
+            users[ch] = []
+            chunk_seq.append(ch)
+        users[ch].append(s)
+
+    with ExitStack() as ctx:
+        const = ctx.enter_context(tc.tile_pool(name="const", bufs=1))
+        rawp = ctx.enter_context(tc.tile_pool(name="rawp", bufs=NB))
+        grp = ctx.enter_context(tc.tile_pool(name="grp", bufs=GB))
+        cod = ctx.enter_context(tc.tile_pool(name="cod", bufs=CB))
+        tmp = ctx.enter_context(tc.tile_pool(name="tmp", bufs=TB))
+        stg = ctx.enter_context(tc.tile_pool(name="stg", bufs=SB))
+        psum = ctx.enter_context(tc.psum_pool(name="psum", bufs=1))
+        if MANUAL:
+            ctx.enter_context(tc.manual_schedule())
+
+        raw = {}
+
+        def load_chunk(ch):
+            g, c = divmod(ch, 4)
+            t = rawp.tile([P, 4, 2048], BF16, name="raw%d" % ch, tag="raw")
+            raw[ch] = t
+            src = qkv_w[512 * c:512 * (c + 1), 2048 * g:2048 * (g + 1)].rearrange("(p t) w -> p t w", t=4)
+            return t, src
+
+        x_sb = const.tile([P, 4096], BF16, name="x_sb")
+        rp = const.tile([P, 2, 64, 2], BF16, name="rp")
+        t0, src0 = load_chunk(chunk_seq[0])
+        nc.sync.dma_start(out=t0[:, :, 0:512], in_=src0[:, :, 0:512])
+        nc.sync.dma_start(out=t0[:, :, 512:1024], in_=src0[:, :, 512:1024])
+        for b in range(2):
+            nc.sync.dma_start(out=x_sb[b:P:2, :], in_=x[b].rearrange("(i e) k -> i (e k)", e=2))
+        for b in range(2):
+            nc.sync.dma_start(out=rp[b:P:2].rearrange("p e j r -> p (e j r)"),
+                              in_=rope.rearrange("(i e) o d -> i (e o d)", e=2))
+        nc.sync.dma_start(out=t0[:, :, 1024:2048], in_=src0[:, :, 1024:2048])
+        for k in range(1, NB):
+            t, src = load_chunk(chunk_seq[k])
+            nc.sync.dma_start(out=t[:], in_=src)
+        next_load = NB
+
+        ident = const.tile([P, P], F32, name="ident")
+        make_identity(nc, ident[:])
+        tbl = const.tile([P, 2, 2, 64, 2], F32, name="tbl")
+        nc.gpsimd.tensor_copy(out=tbl[:, :, 0, :, :], in_=rp[:])
+        nc.gpsimd.tensor_scalar(out=tbl[:, :, 1, :, 0], in0=rp[:, :, :, 1], scalar1=-1.0, scalar2=0.0, op0=MULT, op1=ADD)
+        nc.gpsimd.tensor_copy(out=tbl[:, :, 1, :, 1], in_=rp[:, :, :, 0])
+
+        xw = x_sb[:].bitcast(F32)
+        gx = const.tile([P, 4096], BF16, name="gx", align_bytes=64)
+        gxf = gx[:].bitcast(F32)
+        xc = const.tile([P, 1024], U32, name="xc", align_bytes=64)
+        xs = const.tile([P, 1024], U8, name="xs", align_bytes=64)
+        xt = []
+        for c in range(4):
+            t = psum.tile([P, 2, 2, P], F32, name="xt%d" % c, tag="bank%d" % (2 * c))
+            xt.append(t)
+            for e in range(2):
+                for u in range(2):
+                    lo = 1024 * e + 256 * c + u
+                    nc.tensor.transpose(t[:, e, u, :], xw[:, lo:lo + 255:2], ident[:])
+
+        def x_path():
+            for c in range(4):
+                dst = gxf[:, 512 * c:512 * (c + 1)].rearrange("p (e r u) -> p e r u", e=2, u=2)
+                srcv = xt[c][:].rearrange("p e u r -> p e r u")
+                if c % 2 == 0:
+                    nc.vector.tensor_copy(out=dst, in_=srcv)
+                else:
+                    nc.scalar.copy(out=dst, in_=srcv)
+            for c in range(4):
+                nc.vector.quantize_mx(out=xc[:, 256 * c:256 * (c + 1)].bitcast(FP8X4),
+                                      scales=xs[:, 256 * c:256 * (c + 1)],
+                                      in_=gx[:, 1024 * c:1024 * (c + 1)])
+
+        grouped = {}
+        codes = {}
+        acc = {}
+
+        def regroup(s):
+            g, c, nb = order[s]
+            t = grp.tile([P, 512, 4], BF16, name="grouped%d" % s, tag="grouped", align_bytes=64)
+            grouped[s] = t
+            srcv = raw[4 * g + c][:, :, 512 * nb:512 * (nb + 1)].rearrange("p t (c i) -> p c t i", i=4)
+            dst = t[:].rearrange("p (c i) t -> p c t i", i=4)
+            if ENG[s] == "V":
+                nc.vector.tensor_copy(out=dst, in_=srcv)
+            else:
+                nc.scalar.copy(out=dst, in_=srcv)
+
+        def quantise(s):
+            w = cod.tile([P, 512], U32, name="words%d" % s, tag="words", align_bytes=64)
+            sc = cod.tile([P, 512], U8, name="scales%d" % s, tag="scales", align_bytes=64)
+            codes[s] = (w, sc)
+            nc.vector.quantize_mx(out=w[:].bitcast(FP8X4), scales=sc[:],
+                                  in_=grouped[s][:].rearrange("p w t -> p (w t)"))
+
+        def multiply(s):
+            g, c, nb = order[s]
+            w, sc = codes[s]
+            for e in range(2):
+                if c == 0:
+                    acc[(g, nb, e)] = psum.tile([P, 512], F32, name="acc%d_%d_%d" % (g, nb, e), tag="bank%d" % (2 * nb + e))
+                lo = 256 * c + 128 * e
+                nc.tensor.matmul_mx(out=acc[(g, nb, e)][:],
+                                    lhsT=xc[:, lo:lo + 128].bitcast(FP8X4), lhsT_scale=xs[:, lo:lo + 128],
+                                    rhs=w[:].bitcast(FP8X4), rhs_scale=sc[:],
+                                    start=(c == 0), stop=(c == 3))
+
+        def evacuate(g, nb):
+            stage = stg.tile([P, 4, 2, P], F32, name="stage%d_%d" % (g, nb), tag="stage")
+            if g < 2:
+                prods = []
+                for e in range(2):
+                    pr = tmp.tile([P, 2, 4, 64, 2], F32, name="prod%d_%d_%d" % (g, nb, e), tag="prod")
+                    prods.append(pr)
+                    in0 = acc[(g, nb, e)][:].rearrange("p (h j r) -> p r h j", h=4, r=2).unsqueeze(4).to_broadcast([P, 2, 4, 64, 2])
+                    in1 = tbl[:, e].unsqueeze(2).to_broadcast([P, 2, 4, 64, 2])
+                    nc.vector.tensor_tensor(out=pr[:], in0=in0, in1=in1, op=MULT)
+                for e in range(2):
+                    a = prods[e][:, 0].rearrange("p h j r -> p h (j r)")
+                    bb = prods[e][:, 1].rearrange("p h j r -> p h (j r)")
+                    if ADD_ENGINE == "V":
+                        nc.vector.tensor_tensor(out=stage[:, :, e, :], in0=a, in1=bb, op=ADD)
+                    else:
+                        nc.gpsimd.tensor_tensor(out=stage[:, :, e, :], in0=a, in1=bb, op=ADD)
+            else:
+                for e in range(2):
+                    srcv = acc[(g, nb, e)][:].rearrange("p (h d) -> p h d", h=4)
+                    if e == 0:
+                        nc.vector.tensor_copy(out=stage[:, :, e, :], in_=srcv)
+                    else:
+                        nc.scalar.copy(out=stage[:, :, e, :], in_=srcv)
+            for b in range(2):
+                nc.sync.dma_start(out=outs[g][b, 4 * nb:4 * nb + 4].rearrange("h (i e) d -> i h (e d)", e=2),
+                                  in_=stage[b:P:2].rearrange("p h e d -> p h (e d)"))
+
+        pend_m = []
+        pend_e = []
+        n_evac = 0
+        x_done = False
+        for s in range(n_sub + LQ + LE + 8):
+            if s < n_sub:
+                regroup(s)
+                while next_load < 12 and max(users[chunk_seq[next_load - NB]]) <= s:
+                    t, src = load_chunk(chunk_seq[next_load])
+                    nc.sync.dma_start(out=t[:], in_=src)
+                    next_load += 1
+            if s == X_AFTER:
+                x_path()
+                x_done = True
+            q = s - LQ
+            if 0 <= q < n_sub:
+                quantise(q)
+                pend_m.append(q)
+            if x_done:
+                for m in pend_m:
+                    multiply(m)
+                    pend_e.append((m, s + LE))
+                pend_m = []
+            while n_evac < len(pend_e) and pend_e[n_evac][1] <= s:
+                m = pend_e[n_evac][0]
+                n_evac += 1
+                g, c, nb = order[m]
+                if last_of[(g, nb)] == m:
+                    evacuate(g, nb)

@@ -14,17 +14,16 @@ ADD = mybir.AluOpType.add
 FLOPS = 2 * 256 * 2048 * 6144
 
 P = 128
-NB = 6
-GB = 6
+NB = 5
+GB = 8
 CB = 16
-TB = 3
+TB = 4
 SB = 4
 LQ = 1
-LE = 1
 X_AFTER = 1
-ENG = "VSSVVSVSVSVSVSVS" + "SSSSSSSSSVSVSVSS" + "SSSSSSSSVSSVSVSV"
+ENG = "VSVSVSVSVSVSVSVS" + "VSSSSSSSSVSVSVSV" + "SSSSSSSSVSSVVVSV"
 HYBRID = (False, False, True)
-ADD_ENGINE = "V"
+N_G = 6
 MANUAL = True
 
 
@@ -84,19 +83,26 @@ def tile_attention_pa_kernel(tc, x, rope, qkv_w, out_0, out_1, out_2):
 
         x_sb = const.tile([P, 4096], BF16, name="x_sb")
         rp = const.tile([P, 2, 64, 2], BF16, name="rp")
-        t0, src0 = load_chunk(chunk_seq[0])
-        nc.sync.dma_start(out=t0[:, :, 0:512], in_=src0[:, :, 0:512])
-        nc.sync.dma_start(out=t0[:, :, 512:1024], in_=src0[:, :, 512:1024])
+        first = []
+
+        def load_first(nb):
+            t = const.tile([P, 4, 512], BF16, name="first%d" % nb)
+            first.append(t)
+            nc.sync.dma_start(out=t[:], in_=qkv_w[0:512, 512 * nb:512 * (nb + 1)].rearrange("(p t) w -> p t w", t=4))
+
+        load_first(0)
+        load_first(1)
         for b in range(2):
             nc.sync.dma_start(out=x_sb[b:P:2, :], in_=x[b].rearrange("(i e) k -> i (e k)", e=2))
+        load_first(2)
+        load_first(3)
         for b in range(2):
             nc.sync.dma_start(out=rp[b:P:2].rearrange("p e j r -> p (e j r)"),
                               in_=rope.rearrange("(i e) o d -> i (e o d)", e=2))
-        nc.sync.dma_start(out=t0[:, :, 1024:2048], in_=src0[:, :, 1024:2048])
-        for k in range(1, NB):
+        for k in range(1, NB + 1):
             t, src = load_chunk(chunk_seq[k])
             nc.sync.dma_start(out=t[:], in_=src)
-        next_load = NB
+        next_load = NB + 1
 
         ident = const.tile([P, P], F32, name="ident")
         make_identity(nc, ident[:])
@@ -140,7 +146,10 @@ def tile_attention_pa_kernel(tc, x, rope, qkv_w, out_0, out_1, out_2):
             g, c, nb = order[s]
             t = grp.tile([P, 512, 4], BF16, name="grouped%d" % s, tag="grouped", align_bytes=64)
             grouped[s] = t
-            srcv = raw[4 * g + c][:, :, 512 * nb:512 * (nb + 1)].rearrange("p t (c i) -> p c t i", i=4)
+            if g == 0 and c == 0:
+                srcv = first[nb][:].rearrange("p t (c i) -> p c t i", i=4)
+            else:
+                srcv = raw[4 * g + c][:, :, 512 * nb:512 * (nb + 1)].rearrange("p t (c i) -> p c t i", i=4)
             dst = t[:].rearrange("p (c i) t -> p c t i", i=4)
             if ENG[s] == "V":
                 nc.vector.tensor_copy(out=dst, in_=srcv)
@@ -166,42 +175,57 @@ def tile_attention_pa_kernel(tc, x, rope, qkv_w, out_0, out_1, out_2):
                                     rhs=w[:].bitcast(FP8X4), rhs_scale=sc[:],
                                     start=(c == 0), stop=(c == 3))
 
-        def evacuate(g, nb):
-            stage = stg.tile([P, 4, 2, P], F32, name="stage%d_%d" % (g, nb), tag="stage")
-            if g < 2:
-                prods = []
-                for e in range(2):
-                    pr = tmp.tile([P, 2, 4, 64, 2], F32, name="prod%d_%d_%d" % (g, nb, e), tag="prod")
-                    prods.append(pr)
-                    in0 = acc[(g, nb, e)][:].rearrange("p (h j r) -> p r h j", h=4, r=2).unsqueeze(4).to_broadcast([P, 2, 4, 64, 2])
-                    in1 = tbl[:, e].unsqueeze(2).to_broadcast([P, 2, 4, 64, 2])
-                    nc.vector.tensor_tensor(out=pr[:], in0=in0, in1=in1, op=MULT)
-                for e in range(2):
-                    a = prods[e][:, 0].rearrange("p h j r -> p h (j r)")
-                    bb = prods[e][:, 1].rearrange("p h j r -> p h (j r)")
-                    if ADD_ENGINE == "V":
-                        nc.vector.tensor_tensor(out=stage[:, :, e, :], in0=a, in1=bb, op=ADD)
-                    else:
-                        nc.gpsimd.tensor_tensor(out=stage[:, :, e, :], in0=a, in1=bb, op=ADD)
-            else:
-                for e in range(2):
-                    srcv = acc[(g, nb, e)][:].rearrange("p (h d) -> p h d", h=4)
-                    if e == 0:
-                        nc.vector.tensor_copy(out=stage[:, :, e, :], in_=srcv)
-                    else:
-                        nc.scalar.copy(out=stage[:, :, e, :], in_=srcv)
+        def store(g, nb, stage):
             for b in range(2):
                 nc.sync.dma_start(out=outs[g][b, 4 * nb:4 * nb + 4].rearrange("h (i e) d -> i h (e d)", e=2),
                                   in_=stage[b:P:2].rearrange("p h e d -> p h (e d)"))
 
+        def products(g, nb, e):
+            pr = tmp.tile([P, 2, 4, 64, 2], F32, name="prod%d_%d_%d" % (g, nb, e), tag="prod")
+            in0 = acc[(g, nb, e)][:].rearrange("p (h j r) -> p r h j", h=4, r=2).unsqueeze(4).to_broadcast([P, 2, 4, 64, 2])
+            in1 = tbl[:, e].unsqueeze(2).to_broadcast([P, 2, 4, 64, 2])
+            nc.vector.tensor_tensor(out=pr[:], in0=in0, in1=in1, op=MULT)
+            return pr
+
+        def add_products(engine, stage, e, pr):
+            engine.tensor_tensor(out=stage[:, :, e, :], in0=pr[:, 0].rearrange("p h j r -> p h (j r)"),
+                                 in1=pr[:, 1].rearrange("p h j r -> p h (j r)"), op=ADD)
+
+        def rope_burst(g):
+            late = []
+            n = 0
+            for nb in range(4):
+                stage = stg.tile([P, 4, 2, P], F32, name="stage%d_%d" % (g, nb), tag="stage")
+                for e in range(2):
+                    pr = products(g, nb, e)
+                    if n < N_G:
+                        add_products(nc.gpsimd, stage, e, pr)
+                    else:
+                        late.append((nb, stage, e, pr))
+                    n += 1
+                if n <= N_G:
+                    store(g, nb, stage)
+            for nb, stage, e, pr in late:
+                add_products(nc.vector, stage, e, pr)
+                if e == 1:
+                    store(g, nb, stage)
+
+        def copy_out(g, nb):
+            stage = stg.tile([P, 4, 2, P], F32, name="stage%d_%d" % (g, nb), tag="stage")
+            for e in range(2):
+                srcv = acc[(g, nb, e)][:].rearrange("p (h d) -> p h d", h=4)
+                if nb == 3 and e == 0:
+                    nc.vector.tensor_copy(out=stage[:, :, e, :], in_=srcv)
+                else:
+                    nc.scalar.copy(out=stage[:, :, e, :], in_=srcv)
+            store(g, nb, stage)
+
         pend_m = []
-        pend_e = []
-        n_evac = 0
         x_done = False
-        for s in range(n_sub + LQ + LE + 8):
+        for s in range(n_sub + LQ + 2):
             if s < n_sub:
                 regroup(s)
-                while next_load < 12 and max(users[chunk_seq[next_load - NB]]) <= s:
+                while next_load < 12 and (next_load - NB < 1 or max(users[chunk_seq[next_load - NB]]) <= s):
                     t, src = load_chunk(chunk_seq[next_load])
                     nc.sync.dma_start(out=t[:], in_=src)
                     next_load += 1
@@ -215,11 +239,9 @@ def tile_attention_pa_kernel(tc, x, rope, qkv_w, out_0, out_1, out_2):
             if x_done:
                 for m in pend_m:
                     multiply(m)
-                    pend_e.append((m, s + LE))
+                    g, c, nb = order[m]
+                    if g < 2 and m == 16 * g + 15:
+                        rope_burst(g)
+                    if g == 2 and last_of[(g, nb)] == m:
+                        copy_out(g, nb)
                 pend_m = []
-            while n_evac < len(pend_e) and pend_e[n_evac][1] <= s:
-                m = pend_e[n_evac][0]
-                n_evac += 1
-                g, c, nb = order[m]
-                if last_of[(g, nb)] == m:
-                    evacuate(g, nb)

@@ -14,13 +14,12 @@ ADD = mybir.AluOpType.add
 FLOPS = 2 * 256 * 2048 * 6144
 
 P = 128
-NB = 5
+NB = 6
 GB = 8
 CB = 16
 TB = 4
 SB = 4
 LQ = 1
-X_AFTER = 1
 ENG = "VSVSVSVSVSVSVSVS" + "VSSSSSSSSVSVSVSV" + "SSSSSSSSVSSVVVSV"
 HYBRID = (False, False, True)
 N_G = 6
@@ -83,26 +82,16 @@ def tile_attention_pa_kernel(tc, x, rope, qkv_w, out_0, out_1, out_2):
 
         x_sb = const.tile([P, 4096], BF16, name="x_sb")
         rp = const.tile([P, 2, 64, 2], BF16, name="rp")
-        first = []
-
-        def load_first(nb):
-            t = const.tile([P, 4, 512], BF16, name="first%d" % nb)
-            first.append(t)
-            nc.sync.dma_start(out=t[:], in_=qkv_w[0:512, 512 * nb:512 * (nb + 1)].rearrange("(p t) w -> p t w", t=4))
-
-        load_first(0)
-        load_first(1)
         for b in range(2):
             nc.sync.dma_start(out=x_sb[b:P:2, :], in_=x[b].rearrange("(i e) k -> i (e k)", e=2))
-        load_first(2)
-        load_first(3)
-        for b in range(2):
-            nc.sync.dma_start(out=rp[b:P:2].rearrange("p e j r -> p (e j r)"),
-                              in_=rope.rearrange("(i e) o d -> i (e o d)", e=2))
-        for k in range(1, NB + 1):
+        for k in range(NB):
             t, src = load_chunk(chunk_seq[k])
             nc.sync.dma_start(out=t[:], in_=src)
-        next_load = NB + 1
+            if k == 1:
+                for b in range(2):
+                    nc.sync.dma_start(out=rp[b:P:2].rearrange("p e j r -> p (e j r)"),
+                                      in_=rope.rearrange("(i e) o d -> i (e o d)", e=2))
+        next_load = NB
 
         ident = const.tile([P, P], F32, name="ident")
         make_identity(nc, ident[:])
@@ -146,10 +135,7 @@ def tile_attention_pa_kernel(tc, x, rope, qkv_w, out_0, out_1, out_2):
             g, c, nb = order[s]
             t = grp.tile([P, 512, 4], BF16, name="grouped%d" % s, tag="grouped", align_bytes=64)
             grouped[s] = t
-            if g == 0 and c == 0:
-                srcv = first[nb][:].rearrange("p t (c i) -> p c t i", i=4)
-            else:
-                srcv = raw[4 * g + c][:, :, 512 * nb:512 * (nb + 1)].rearrange("p t (c i) -> p c t i", i=4)
+            srcv = raw[4 * g + c][:, :, 512 * nb:512 * (nb + 1)].rearrange("p t (c i) -> p c t i", i=4)
             dst = t[:].rearrange("p (c i) t -> p c t i", i=4)
             if ENG[s] == "V":
                 nc.vector.tensor_copy(out=dst, in_=srcv)
@@ -220,28 +206,20 @@ def tile_attention_pa_kernel(tc, x, rope, qkv_w, out_0, out_1, out_2):
                     nc.scalar.copy(out=stage[:, :, e, :], in_=srcv)
             store(g, nb, stage)
 
-        pend_m = []
-        x_done = False
-        for s in range(n_sub + LQ + 2):
+        x_path()
+        for s in range(n_sub + LQ):
             if s < n_sub:
                 regroup(s)
-                while next_load < 12 and (next_load - NB < 1 or max(users[chunk_seq[next_load - NB]]) <= s):
+                while next_load < 12 and max(users[chunk_seq[next_load - NB]]) <= s:
                     t, src = load_chunk(chunk_seq[next_load])
                     nc.sync.dma_start(out=t[:], in_=src)
                     next_load += 1
-            if s == X_AFTER:
-                x_path()
-                x_done = True
-            q = s - LQ
-            if 0 <= q < n_sub:
-                quantise(q)
-                pend_m.append(q)
-            if x_done:
-                for m in pend_m:
-                    multiply(m)
-                    g, c, nb = order[m]
-                    if g < 2 and m == 16 * g + 15:
-                        rope_burst(g)
-                    if g == 2 and last_of[(g, nb)] == m:
-                        copy_out(g, nb)
-                pend_m = []
+            m = s - LQ
+            if m >= 0:
+                quantise(m)
+                multiply(m)
+                g, c, nb = order[m]
+                if g < 2 and m == 16 * g + 15:
+                    rope_burst(g)
+                if g == 2 and last_of[(g, nb)] == m:
+                    copy_out(g, nb)

@@ -15,14 +15,14 @@ FLOPS = 2 * 256 * 2048 * 6144
 
 P = 128
 NB = 6
-GB = 8
-CB = 16
-TB = 4
+GB = 4
+CB = 6
+TB = 3
 SB = 4
-LQ = 1
-ENG = "VSVSVSVSVSVSVSVS" + "VSSSSSSSSVSVSVSV" + "SSSSSSSSVSSVVVSV"
+LQ = 2
+ENG = "VSVSVSVSVSVSVSVS" + "VSSSSSSSSVSVSVSV" + "SSSSSSSSSVSVSVVV"
 HYBRID = (False, False, True)
-N_G = 6
+N_G = 3
 MANUAL = True
 
 
@@ -122,10 +122,10 @@ def tile_attention_pa_kernel(tc, x, rope, qkv_w, out_0, out_1, out_2):
                     nc.vector.tensor_copy(out=dst, in_=srcv)
                 else:
                     nc.scalar.copy(out=dst, in_=srcv)
-            for c in range(4):
-                nc.vector.quantize_mx(out=xc[:, 256 * c:256 * (c + 1)].bitcast(FP8X4),
-                                      scales=xs[:, 256 * c:256 * (c + 1)],
-                                      in_=gx[:, 1024 * c:1024 * (c + 1)])
+            for c in range(2):
+                nc.vector.quantize_mx(out=xc[:, 512 * c:512 * (c + 1)].bitcast(FP8X4),
+                                      scales=xs[:, 512 * c:512 * (c + 1)],
+                                      in_=gx[:, 2048 * c:2048 * (c + 1)])
 
         grouped = {}
         codes = {}
@@ -133,32 +133,34 @@ def tile_attention_pa_kernel(tc, x, rope, qkv_w, out_0, out_1, out_2):
 
         def regroup(s):
             g, c, nb = order[s]
-            t = grp.tile([P, 512, 4], BF16, name="grouped%d" % s, tag="grouped", align_bytes=64)
-            grouped[s] = t
+            if s % 2 == 0:
+                grouped[s // 2] = grp.tile([P, 1024, 4], BF16, name="grouped%d" % (s // 2), tag="grouped", align_bytes=64)
+            half = 512 * (s % 2)
             srcv = raw[4 * g + c][:, :, 512 * nb:512 * (nb + 1)].rearrange("p t (c i) -> p c t i", i=4)
-            dst = t[:].rearrange("p (c i) t -> p c t i", i=4)
+            dst = grouped[s // 2][:, half:half + 512, :].rearrange("p (c i) t -> p c t i", i=4)
             if ENG[s] == "V":
                 nc.vector.tensor_copy(out=dst, in_=srcv)
             else:
                 nc.scalar.copy(out=dst, in_=srcv)
 
-        def quantise(s):
-            w = cod.tile([P, 512], U32, name="words%d" % s, tag="words", align_bytes=64)
-            sc = cod.tile([P, 512], U8, name="scales%d" % s, tag="scales", align_bytes=64)
-            codes[s] = (w, sc)
+        def quantise(i):
+            w = cod.tile([P, 1024], U32, name="words%d" % i, tag="words", align_bytes=64)
+            sc = cod.tile([P, 1024], U8, name="scales%d" % i, tag="scales", align_bytes=64)
+            codes[i] = (w, sc)
             nc.vector.quantize_mx(out=w[:].bitcast(FP8X4), scales=sc[:],
-                                  in_=grouped[s][:].rearrange("p w t -> p (w t)"))
+                                  in_=grouped[i][:].rearrange("p w t -> p (w t)"))
 
         def multiply(s):
             g, c, nb = order[s]
-            w, sc = codes[s]
+            w, sc = codes[s // 2]
+            half = 512 * (s % 2)
             for e in range(2):
                 if c == 0:
                     acc[(g, nb, e)] = psum.tile([P, 512], F32, name="acc%d_%d_%d" % (g, nb, e), tag="bank%d" % (2 * nb + e))
                 lo = 256 * c + 128 * e
                 nc.tensor.matmul_mx(out=acc[(g, nb, e)][:],
                                     lhsT=xc[:, lo:lo + 128].bitcast(FP8X4), lhsT_scale=xs[:, lo:lo + 128],
-                                    rhs=w[:].bitcast(FP8X4), rhs_scale=sc[:],
+                                    rhs=w[:, half:half + 512].bitcast(FP8X4), rhs_scale=sc[:, half:half + 512],
                                     start=(c == 0), stop=(c == 3))
 
         def store(g, nb, stage):
@@ -166,35 +168,31 @@ def tile_attention_pa_kernel(tc, x, rope, qkv_w, out_0, out_1, out_2):
                 nc.sync.dma_start(out=outs[g][b, 4 * nb:4 * nb + 4].rearrange("h (i e) d -> i h (e d)", e=2),
                                   in_=stage[b:P:2].rearrange("p h e d -> p h (e d)"))
 
-        def products(g, nb, e):
-            pr = tmp.tile([P, 2, 4, 64, 2], F32, name="prod%d_%d_%d" % (g, nb, e), tag="prod")
-            in0 = acc[(g, nb, e)][:].rearrange("p (h j r) -> p r h j", h=4, r=2).unsqueeze(4).to_broadcast([P, 2, 4, 64, 2])
-            in1 = tbl[:, e].unsqueeze(2).to_broadcast([P, 2, 4, 64, 2])
-            nc.vector.tensor_tensor(out=pr[:], in0=in0, in1=in1, op=MULT)
+        def products(g, nb):
+            pr = tmp.tile([P, 2, 2, 4, 64, 2], F32, name="prod%d_%d" % (g, nb), tag="prod")
+            for e in range(2):
+                in0 = acc[(g, nb, e)][:].rearrange("p (h j r) -> p r h j", h=4, r=2).unsqueeze(4).to_broadcast([P, 2, 4, 64, 2])
+                in1 = tbl[:, e].unsqueeze(2).to_broadcast([P, 2, 4, 64, 2])
+                nc.vector.tensor_tensor(out=pr[:, e], in0=in0, in1=in1, op=MULT)
             return pr
 
-        def add_products(engine, stage, e, pr):
-            engine.tensor_tensor(out=stage[:, :, e, :], in0=pr[:, 0].rearrange("p h j r -> p h (j r)"),
-                                 in1=pr[:, 1].rearrange("p h j r -> p h (j r)"), op=ADD)
+        def add_products(engine, stage, pr):
+            engine.tensor_tensor(out=stage[:], in0=pr[:, :, 0].rearrange("p e h j r -> p h e (j r)"),
+                                 in1=pr[:, :, 1].rearrange("p e h j r -> p h e (j r)"), op=ADD)
 
         def rope_burst(g):
             late = []
-            n = 0
             for nb in range(4):
                 stage = stg.tile([P, 4, 2, P], F32, name="stage%d_%d" % (g, nb), tag="stage")
-                for e in range(2):
-                    pr = products(g, nb, e)
-                    if n < N_G:
-                        add_products(nc.gpsimd, stage, e, pr)
-                    else:
-                        late.append((nb, stage, e, pr))
-                    n += 1
-                if n <= N_G:
+                pr = products(g, nb)
+                if nb < N_G:
+                    add_products(nc.gpsimd, stage, pr)
                     store(g, nb, stage)
-            for nb, stage, e, pr in late:
-                add_products(nc.vector, stage, e, pr)
-                if e == 1:
-                    store(g, nb, stage)
+                else:
+                    late.append((nb, stage, pr))
+            for nb, stage, pr in late:
+                add_products(nc.vector, stage, pr)
+                store(g, nb, stage)
 
         def copy_out(g, nb):
             stage = stg.tile([P, 4, 2, P], F32, name="stage%d_%d" % (g, nb), tag="stage")
@@ -214,12 +212,14 @@ def tile_attention_pa_kernel(tc, x, rope, qkv_w, out_0, out_1, out_2):
                     t, src = load_chunk(chunk_seq[next_load])
                     nc.sync.dma_start(out=t[:], in_=src)
                     next_load += 1
-            m = s - LQ
-            if m >= 0:
-                quantise(m)
-                multiply(m)
-                g, c, nb = order[m]
-                if g < 2 and m == 16 * g + 15:
-                    rope_burst(g)
-                if g == 2 and last_of[(g, nb)] == m:
-                    copy_out(g, nb)
+            t = s - LQ
+            if t >= 0 and t % 2 == 1:
+                quantise(t // 2)
+                for m in (t - 1, t):
+                    multiply(m)
+                for m in (t - 1, t):
+                    g, c, nb = order[m]
+                    if g < 2 and m == 16 * g + 15:
+                        rope_burst(g)
+                    if g == 2 and last_of[(g, nb)] == m:
+                        copy_out(g, nb)

@@ -15,15 +15,15 @@ FLOPS = 2 * 256 * 2048 * 6144
 
 P = 128
 NB = 6
-GB = 4
-CB = 6
-TB = 3
+GB = 8
+CB = 16
+TB = 4
 SB = 4
-LQ = 2
-ENG = "VSVSVSVSVSVSVSVS" + "VSSSSSSSSVSVSVSV" + "SSSSSSSSSVSVSVVV"
+LQ = 1
+ENG = "VSVSVSVSVSVSVSVS" + "VSSSSSSSSVSVSVSV" + "SSSSSSSSVSSVVVSV"
 HYBRID = (False, False, True)
-N_G = 3
-MANUAL = True
+N_G = 6
+MANUAL = False
 
 
 def sub_block_order():
@@ -122,10 +122,10 @@ def tile_attention_pa_kernel(tc, x, rope, qkv_w, out_0, out_1, out_2):
                     nc.vector.tensor_copy(out=dst, in_=srcv)
                 else:
                     nc.scalar.copy(out=dst, in_=srcv)
-            for c in range(2):
-                nc.vector.quantize_mx(out=xc[:, 512 * c:512 * (c + 1)].bitcast(FP8X4),
-                                      scales=xs[:, 512 * c:512 * (c + 1)],
-                                      in_=gx[:, 2048 * c:2048 * (c + 1)])
+            for c in range(4):
+                nc.vector.quantize_mx(out=xc[:, 256 * c:256 * (c + 1)].bitcast(FP8X4),
+                                      scales=xs[:, 256 * c:256 * (c + 1)],
+                                      in_=gx[:, 1024 * c:1024 * (c + 1)])
 
         grouped = {}
         codes = {}
@@ -133,34 +133,32 @@ def tile_attention_pa_kernel(tc, x, rope, qkv_w, out_0, out_1, out_2):
 
         def regroup(s):
             g, c, nb = order[s]
-            if s % 2 == 0:
-                grouped[s // 2] = grp.tile([P, 1024, 4], BF16, name="grouped%d" % (s // 2), tag="grouped", align_bytes=64)
-            half = 512 * (s % 2)
+            t = grp.tile([P, 512, 4], BF16, name="grouped%d" % s, tag="grouped", align_bytes=64)
+            grouped[s] = t
             srcv = raw[4 * g + c][:, :, 512 * nb:512 * (nb + 1)].rearrange("p t (c i) -> p c t i", i=4)
-            dst = grouped[s // 2][:, half:half + 512, :].rearrange("p (c i) t -> p c t i", i=4)
+            dst = t[:].rearrange("p (c i) t -> p c t i", i=4)
             if ENG[s] == "V":
                 nc.vector.tensor_copy(out=dst, in_=srcv)
             else:
                 nc.scalar.copy(out=dst, in_=srcv)
 
-        def quantise(i):
-            w = cod.tile([P, 1024], U32, name="words%d" % i, tag="words", align_bytes=64)
-            sc = cod.tile([P, 1024], U8, name="scales%d" % i, tag="scales", align_bytes=64)
-            codes[i] = (w, sc)
+        def quantise(s):
+            w = cod.tile([P, 512], U32, name="words%d" % s, tag="words", align_bytes=64)
+            sc = cod.tile([P, 512], U8, name="scales%d" % s, tag="scales", align_bytes=64)
+            codes[s] = (w, sc)
             nc.vector.quantize_mx(out=w[:].bitcast(FP8X4), scales=sc[:],
-                                  in_=grouped[i][:].rearrange("p w t -> p (w t)"))
+                                  in_=grouped[s][:].rearrange("p w t -> p (w t)"))
 
         def multiply(s):
             g, c, nb = order[s]
-            w, sc = codes[s // 2]
-            half = 512 * (s % 2)
+            w, sc = codes[s]
             for e in range(2):
                 if c == 0:
                     acc[(g, nb, e)] = psum.tile([P, 512], F32, name="acc%d_%d_%d" % (g, nb, e), tag="bank%d" % (2 * nb + e))
                 lo = 256 * c + 128 * e
                 nc.tensor.matmul_mx(out=acc[(g, nb, e)][:],
                                     lhsT=xc[:, lo:lo + 128].bitcast(FP8X4), lhsT_scale=xs[:, lo:lo + 128],
-                                    rhs=w[:, half:half + 512].bitcast(FP8X4), rhs_scale=sc[:, half:half + 512],
+                                    rhs=w[:].bitcast(FP8X4), rhs_scale=sc[:],
                                     start=(c == 0), stop=(c == 3))
 
         def store(g, nb, stage):
@@ -168,31 +166,35 @@ def tile_attention_pa_kernel(tc, x, rope, qkv_w, out_0, out_1, out_2):
                 nc.sync.dma_start(out=outs[g][b, 4 * nb:4 * nb + 4].rearrange("h (i e) d -> i h (e d)", e=2),
                                   in_=stage[b:P:2].rearrange("p h e d -> p h (e d)"))
 
-        def products(g, nb):
-            pr = tmp.tile([P, 2, 2, 4, 64, 2], F32, name="prod%d_%d" % (g, nb), tag="prod")
-            for e in range(2):
-                in0 = acc[(g, nb, e)][:].rearrange("p (h j r) -> p r h j", h=4, r=2).unsqueeze(4).to_broadcast([P, 2, 4, 64, 2])
-                in1 = tbl[:, e].unsqueeze(2).to_broadcast([P, 2, 4, 64, 2])
-                nc.vector.tensor_tensor(out=pr[:, e], in0=in0, in1=in1, op=MULT)
+        def products(g, nb, e):
+            pr = tmp.tile([P, 2, 4, 64, 2], F32, name="prod%d_%d_%d" % (g, nb, e), tag="prod")
+            in0 = acc[(g, nb, e)][:].rearrange("p (h j r) -> p r h j", h=4, r=2).unsqueeze(4).to_broadcast([P, 2, 4, 64, 2])
+            in1 = tbl[:, e].unsqueeze(2).to_broadcast([P, 2, 4, 64, 2])
+            nc.vector.tensor_tensor(out=pr[:], in0=in0, in1=in1, op=MULT)
             return pr
 
-        def add_products(engine, stage, pr):
-            engine.tensor_tensor(out=stage[:], in0=pr[:, :, 0].rearrange("p e h j r -> p h e (j r)"),
-                                 in1=pr[:, :, 1].rearrange("p e h j r -> p h e (j r)"), op=ADD)
+        def add_products(engine, stage, e, pr):
+            engine.tensor_tensor(out=stage[:, :, e, :], in0=pr[:, 0].rearrange("p h j r -> p h (j r)"),
+                                 in1=pr[:, 1].rearrange("p h j r -> p h (j r)"), op=ADD)
 
         def rope_burst(g):
             late = []
+            n = 0
             for nb in range(4):
                 stage = stg.tile([P, 4, 2, P], F32, name="stage%d_%d" % (g, nb), tag="stage")
-                pr = products(g, nb)
-                if nb < N_G:
-                    add_products(nc.gpsimd, stage, pr)
+                for e in range(2):
+                    pr = products(g, nb, e)
+                    if n < N_G:
+                        add_products(nc.gpsimd, stage, e, pr)
+                    else:
+                        late.append((nb, stage, e, pr))
+                    n += 1
+                if n <= N_G:
                     store(g, nb, stage)
-                else:
-                    late.append((nb, stage, pr))
-            for nb, stage, pr in late:
-                add_products(nc.vector, stage, pr)
-                store(g, nb, stage)
+            for nb, stage, e, pr in late:
+                add_products(nc.vector, stage, e, pr)
+                if e == 1:
+                    store(g, nb, stage)
 
         def copy_out(g, nb):
             stage = stg.tile([P, 4, 2, P], F32, name="stage%d_%d" % (g, nb), tag="stage")
@@ -212,14 +214,12 @@ def tile_attention_pa_kernel(tc, x, rope, qkv_w, out_0, out_1, out_2):
                     t, src = load_chunk(chunk_seq[next_load])
                     nc.sync.dma_start(out=t[:], in_=src)
                     next_load += 1
-            t = s - LQ
-            if t >= 0 and t % 2 == 1:
-                quantise(t // 2)
-                for m in (t - 1, t):
-                    multiply(m)
-                for m in (t - 1, t):
-                    g, c, nb = order[m]
-                    if g < 2 and m == 16 * g + 15:
-                        rope_burst(g)
-                    if g == 2 and last_of[(g, nb)] == m:
-                        copy_out(g, nb)
+            m = s - LQ
+            if m >= 0:
+                quantise(m)
+                multiply(m)
+                g, c, nb = order[m]
+                if g < 2 and m == 16 * g + 15:
+                    rope_burst(g)
+                if g == 2 and last_of[(g, nb)] == m:
+                    copy_out(g, nb)

@@ -140,6 +140,8 @@ def tile_attention_pa_kernel(tc, x, rope, qkv_w, out_0, out_1, out_2):
             if ENG[s] == "V":
                 nc.vector.tensor_copy(out=dst, in_=srcv)
             else:
+                srcv = raw[4 * g + c][:, :, 512 * nb:512 * (nb + 1)].rearrange("p t (c i) -> p c t i", i=8)
+                dst = t[:].rearrange("p (c i) t -> p c t i", i=8)
                 nc.scalar.copy(out=dst, in_=srcv)
 
         def quantise(s):

@@ -135,13 +135,11 @@ def tile_attention_pa_kernel(tc, x, rope, qkv_w, out_0, out_1, out_2):
             g, c, nb = order[s]
             t = grp.tile([P, 512, 4], BF16, name="grouped%d" % s, tag="grouped", align_bytes=64)
             grouped[s] = t
-            srcv = raw[4 * g + c][:, :, 512 * nb:512 * (nb + 1)].rearrange("p t (c i) -> p c t i", i=4)
-            dst = t[:].rearrange("p (c i) t -> p c t i", i=4)
+            srcv = raw[4 * g + c][:, :, 512 * nb:512 * (nb + 1)].rearrange("p t (c i) -> p c t i", i=8)
+            dst = t[:].rearrange("p (c i) t -> p c t i", i=8)
             if ENG[s] == "V":
                 nc.vector.tensor_copy(out=dst, in_=srcv)
             else:
-                srcv = raw[4 * g + c][:, :, 512 * nb:512 * (nb + 1)].rearrange("p t (c i) -> p c t i", i=8)
-                dst = t[:].rearrange("p (c i) t -> p c t i", i=8)
                 nc.scalar.copy(out=dst, in_=srcv)
 
         def quantise(s):

@@ -20,10 +20,18 @@ CB = 16
 TB = 4
 SB = 4
 LQ = 1
-ENG = "VSVSVSVSVSVSVSVS" + "VSSSSSSSSVSVSVSV" + "SSSSSSSSVSSVVVSV"
+LEAD = 3
 HYBRID = (False, False, True)
 N_G = 6
-MANUAL = False
+
+
+def who(s):
+    third, i = divmod(s, 16)
+    if third == 0:
+        return "VS"[i % 2]
+    if third == 1:
+        return "P" if i % 3 == 2 else "V" if i >= 9 and i % 3 == 0 else "S"
+    return "P" if i % 3 == 1 and i < 12 else "V" if i >= 9 and i % 2 == 1 else "S"
 
 
 def sub_block_order():
@@ -68,8 +76,6 @@ def tile_attention_pa_kernel(tc, x, rope, qkv_w, out_0, out_1, out_2):
         tmp = ctx.enter_context(tc.tile_pool(name="tmp", bufs=TB))
         stg = ctx.enter_context(tc.tile_pool(name="stg", bufs=SB))
         psum = ctx.enter_context(tc.psum_pool(name="psum", bufs=1))
-        if MANUAL:
-            ctx.enter_context(tc.manual_schedule())
 
         raw = {}
 
@@ -95,6 +101,8 @@ def tile_attention_pa_kernel(tc, x, rope, qkv_w, out_0, out_1, out_2):
 
         ident = const.tile([P, P], F32, name="ident")
         make_identity(nc, ident[:])
+        ident16 = const.tile([P, P], BF16, name="ident16")
+        make_identity(nc, ident16[:])
         tbl = const.tile([P, 2, 2, 64, 2], F32, name="tbl")
         nc.gpsimd.tensor_copy(out=tbl[:, :, 0, :, :], in_=rp[:])
         nc.gpsimd.tensor_scalar(out=tbl[:, :, 1, :, 0], in0=rp[:, :, :, 1], scalar1=-1.0, scalar2=0.0, op0=MULT, op1=ADD)
@@ -130,14 +138,32 @@ def tile_attention_pa_kernel(tc, x, rope, qkv_w, out_0, out_1, out_2):
         grouped = {}
         codes = {}
         acc = {}
+        passed = {}
+
+        def pass_through(s):
+            g, c, nb = order[s]
+            passed[s] = []
+            for h in range(2):
+                t = psum.tile([P, 256, 4], BF16, name="pass%d_%d" % (s, h), tag="bank%d" % (6 + h))
+                passed[s].append(t)
+                lo = 512 * nb + 256 * h
+                for j in range(2):
+                    nc.tensor.matmul(t[:].rearrange("p n t -> p t n")[:, 2 * j:2 * j + 2, :], lhsT=ident16[:],
+                                     rhs=raw[4 * g + c][:, 2 * j:2 * j + 2, lo:lo + 256], start=True, stop=True)
 
         def regroup(s):
             g, c, nb = order[s]
             t = grp.tile([P, 512, 4], BF16, name="grouped%d" % s, tag="grouped", align_bytes=64)
             grouped[s] = t
+            if who(s) == "P":
+                flat = t[:].rearrange("p w t -> p (w t)").bitcast(F32)
+                for h in range(2):
+                    nc.scalar.copy(out=flat[:, 512 * h:512 * (h + 1)],
+                                   in_=passed[s][h][:].rearrange("p n t -> p (n t)").bitcast(F32))
+                return
             srcv = raw[4 * g + c][:, :, 512 * nb:512 * (nb + 1)].rearrange("p t (c i) -> p c t i", i=8)
             dst = t[:].rearrange("p (c i) t -> p c t i", i=8)
-            if ENG[s] == "V":
+            if who(s) == "V":
                 nc.vector.tensor_copy(out=dst, in_=srcv)
             else:
                 nc.scalar.copy(out=dst, in_=srcv)
@@ -154,7 +180,7 @@ def tile_attention_pa_kernel(tc, x, rope, qkv_w, out_0, out_1, out_2):
             w, sc = codes[s]
             for e in range(2):
                 if c == 0:
-                    acc[(g, nb, e)] = psum.tile([P, 512], F32, name="acc%d_%d_%d" % (g, nb, e), tag="bank%d" % (2 * nb + e))
+                    acc[(g, nb, e)] = psum.tile([P, 512], F32, name="acc%d_%d_%d" % (g, nb, e), tag="bank%d" % (2 * ((4 * g + nb) % 3) + e))
                 lo = 256 * c + 128 * e
                 nc.tensor.matmul_mx(out=acc[(g, nb, e)][:],
                                     lhsT=xc[:, lo:lo + 128].bitcast(FP8X4), lhsT_scale=xs[:, lo:lo + 128],
@@ -191,6 +217,8 @@ def tile_attention_pa_kernel(tc, x, rope, qkv_w, out_0, out_1, out_2):
                     n += 1
                 if n <= N_G:
                     store(g, nb, stage)
+                if nb == 0:
+                    release_held()
             for nb, stage, e, pr in late:
                 add_products(nc.vector, stage, e, pr)
                 if e == 1:
@@ -206,9 +234,18 @@ def tile_attention_pa_kernel(tc, x, rope, qkv_w, out_0, out_1, out_2):
                     nc.scalar.copy(out=stage[:, :, e, :], in_=srcv)
             store(g, nb, stage)
 
+        held = []
+
+        def release_held():
+            for k in held:
+                multiply(k)
+            held.clear()
+
         x_path()
         for s in range(n_sub + LQ):
             if s < n_sub:
+                if s + LEAD < n_sub and who(s + LEAD) == "P":
+                    pass_through(s + LEAD)
                 regroup(s)
                 while next_load < 12 and max(users[chunk_seq[next_load - NB]]) <= s:
                     t, src = load_chunk(chunk_seq[next_load])
@@ -217,9 +254,14 @@ def tile_attention_pa_kernel(tc, x, rope, qkv_w, out_0, out_1, out_2):
             m = s - LQ
             if m >= 0:
                 quantise(m)
-                multiply(m)
                 g, c, nb = order[m]
+                if nb == 3 and (g < 2 or c < 2):
+                    held.append(m)
+                else:
+                    multiply(m)
                 if g < 2 and m == 16 * g + 15:
                     rope_burst(g)
                 if g == 2 and last_of[(g, nb)] == m:
                     copy_out(g, nb)
+                    if nb == 0:
+                        release_held()

@@ -20,7 +20,7 @@ CB = 16
 TB = 4
 SB = 4
 LQ = 1
-LEAD = 3
+LEAD = 5
 HYBRID = (False, False, True)
 N_G = 6
 
@@ -29,9 +29,11 @@ def who(s):
     third, i = divmod(s, 16)
     if third == 0:
         return "VS"[i % 2]
+    if i in (3, 6, 10):
+        return "P"
     if third == 1:
-        return "P" if i % 3 == 2 else "V" if i >= 9 and i % 3 == 0 else "S"
-    return "P" if i % 3 == 1 and i < 12 else "V" if i >= 9 and i % 2 == 1 else "S"
+        return "V" if i == 0 or i >= 11 and i % 2 == 1 else "S"
+    return "V" if i >= 9 and i % 2 == 1 else "S"
 
 
 def sub_block_order():
@@ -77,6 +79,7 @@ def tile_attention_pa_kernel(tc, x, rope, qkv_w, out_0, out_1, out_2):
         stg = ctx.enter_context(tc.tile_pool(name="stg", bufs=SB))
         psum = ctx.enter_context(tc.psum_pool(name="psum", bufs=1))
 
+        ctx.enter_context(tc.manual_schedule(engines={mybir.EngineType.PE}))
         raw = {}
 
         def load_chunk(ch):
@@ -242,6 +245,9 @@ def tile_attention_pa_kernel(tc, x, rope, qkv_w, out_0, out_1, out_2):
             held.clear()
 
         x_path()
+        for s in range(LEAD):
+            if who(s) == "P":
+                pass_through(s)
         for s in range(n_sub + LQ):
             if s < n_sub:
                 if s + LEAD < n_sub and who(s + LEAD) == "P":

@@ -18,7 +18,7 @@ NB = 6
 GB = 8
 CB = 16
 TB = 4
-SB = 4
+SB = 6
 LQ = 1
 LEAD = 5
 HYBRID = (False, False, True)
@@ -82,21 +82,31 @@ def tile_attention_pa_kernel(tc, x, rope, qkv_w, out_0, out_1, out_2):
         ctx.enter_context(tc.manual_schedule(engines={mybir.EngineType.PE}))
         raw = {}
 
-        def load_chunk(ch):
+        loads = []
+        for ch in chunk_seq:
             g, c = divmod(ch, 4)
-            t = rawp.tile([P, 4, 2048], BF16, name="raw%d" % ch, tag="raw")
-            raw[ch] = t
-            src = qkv_w[512 * c:512 * (c + 1), 2048 * g:2048 * (g + 1)].rearrange("(p t) w -> p t w", t=4)
-            return t, src
+            width = 2 if g == 0 else 4
+            for first in range(0, 4, width):
+                loads.append((g, c, first, width))
+        load_users = [[s for s, (g, c, nb) in enumerate(order) if (g, c) == (lg, lc) and first <= nb < first + width]
+                      for lg, lc, first, width in loads]
+
+        def load_piece(k):
+            g, c, first, width = loads[k]
+            t = rawp.tile([P, 4, 512 * width], BF16, name="raw%d" % k, tag="raw")
+            lo = 2048 * g + 512 * first
+            nc.sync.dma_start(out=t[:], in_=qkv_w[512 * c:512 * (c + 1), lo:lo + 512 * width].rearrange("(p t) w -> p t w", t=4))
+            for i in range(width):
+                raw[(g, c, first + i)] = t[:, :, 512 * i:512 * (i + 1)]
 
         x_sb = const.tile([P, 4096], BF16, name="x_sb")
         rp = const.tile([P, 2, 64, 2], BF16, name="rp")
-        for b in range(2):
-            nc.sync.dma_start(out=x_sb[b:P:2, :], in_=x[b].rearrange("(i e) k -> i (e k)", e=2))
         for k in range(NB):
-            t, src = load_chunk(chunk_seq[k])
-            nc.sync.dma_start(out=t[:], in_=src)
+            load_piece(k)
             if k == 1:
+                for b in range(2):
+                    nc.sync.dma_start(out=x_sb[b:P:2, :], in_=x[b].rearrange("(i e) k -> i (e k)", e=2))
+            if k == 3:
                 for b in range(2):
                     nc.sync.dma_start(out=rp[b:P:2].rearrange("p e j r -> p (e j r)"),
                                       in_=rope.rearrange("(i e) o d -> i (e o d)", e=2))
@@ -149,10 +159,10 @@ def tile_attention_pa_kernel(tc, x, rope, qkv_w, out_0, out_1, out_2):
             for h in range(2):
                 t = psum.tile([P, 256, 4], BF16, name="pass%d_%d" % (s, h), tag="bank%d" % (6 + h))
                 passed[s].append(t)
-                lo = 512 * nb + 256 * h
+                lo = 256 * h
                 for j in range(2):
                     nc.tensor.matmul(t[:].rearrange("p n t -> p t n")[:, 2 * j:2 * j + 2, :], lhsT=ident16[:],
-                                     rhs=raw[4 * g + c][:, 2 * j:2 * j + 2, lo:lo + 256], start=True, stop=True)
+                                     rhs=raw[(g, c, nb)][:, 2 * j:2 * j + 2, lo:lo + 256], start=True, stop=True)
 
         def regroup(s):
             g, c, nb = order[s]
@@ -164,7 +174,7 @@ def tile_attention_pa_kernel(tc, x, rope, qkv_w, out_0, out_1, out_2):
                     nc.scalar.copy(out=flat[:, 512 * h:512 * (h + 1)],
                                    in_=passed[s][h][:].rearrange("p n t -> p (n t)").bitcast(F32))
                 return
-            srcv = raw[4 * g + c][:, :, 512 * nb:512 * (nb + 1)].rearrange("p t (c i) -> p c t i", i=8)
+            srcv = raw[(g, c, nb)].rearrange("p t (c i) -> p c t i", i=8)
             dst = t[:].rearrange("p (c i) t -> p c t i", i=8)
             if who(s) == "V":
                 nc.vector.tensor_copy(out=dst, in_=srcv)
@@ -253,9 +263,8 @@ def tile_attention_pa_kernel(tc, x, rope, qkv_w, out_0, out_1, out_2):
                 if s + LEAD < n_sub and who(s + LEAD) == "P":
                     pass_through(s + LEAD)
                 regroup(s)
-                while next_load < 12 and max(users[chunk_seq[next_load - NB]]) <= s:
-                    t, src = load_chunk(chunk_seq[next_load])
-                    nc.sync.dma_start(out=t[:], in_=src)
+                while next_load < len(loads) and max(load_users[next_load - NB]) <= s:
+                    load_piece(next_load)
                     next_load += 1
             m = s - LQ
             if m >= 0:

@@ -29,7 +29,7 @@ def who(s):
     third, i = divmod(s, 16)
     if third == 0:
         return "VS"[i % 2]
-    if i in (3, 6, 10):
+    if i in (3, 6, 12):
         return "P"
     if third == 1:
         return "V" if i == 0 or i >= 11 and i % 2 == 1 else "S"
@@ -85,7 +85,7 @@ def tile_attention_pa_kernel(tc, x, rope, qkv_w, out_0, out_1, out_2):
         loads = []
         for ch in chunk_seq:
             g, c = divmod(ch, 4)
-            width = 2 if g == 0 else 4
+            width = 2 if ch < 5 else 4
             for first in range(0, 4, width):
                 loads.append((g, c, first, width))
         load_users = [[s for s, (g, c, nb) in enumerate(order) if (g, c) == (lg, lc) and first <= nb < first + width]
@@ -103,10 +103,10 @@ def tile_attention_pa_kernel(tc, x, rope, qkv_w, out_0, out_1, out_2):
         rp = const.tile([P, 2, 64, 2], BF16, name="rp")
         for k in range(NB):
             load_piece(k)
-            if k == 1:
+            if k == 3:
                 for b in range(2):
                     nc.sync.dma_start(out=x_sb[b:P:2, :], in_=x[b].rearrange("(i e) k -> i (e k)", e=2))
-            if k == 3:
+            if k == 4:
                 for b in range(2):
                     nc.sync.dma_start(out=rp[b:P:2].rearrange("p e j r -> p (e j r)"),
                                       in_=rope.rearrange("(i e) o d -> i (e o d)", e=2))

@@ -20,7 +20,7 @@ CB = 16
 TB = 4
 SB = 6
 LQ = 1
-LEAD = 5
+LEAD = {3: 4, 6: 5, 12: 6}
 HYBRID = (False, False, True)
 N_G = 6
 
@@ -255,13 +255,12 @@ def tile_attention_pa_kernel(tc, x, rope, qkv_w, out_0, out_1, out_2):
             held.clear()
 
         x_path()
-        for s in range(LEAD):
-            if who(s) == "P":
-                pass_through(s)
         for s in range(n_sub + LQ):
             if s < n_sub:
-                if s + LEAD < n_sub and who(s + LEAD) == "P":
-                    pass_through(s + LEAD)
+                for place in LEAD:
+                    ahead = s + LEAD[place]
+                    if ahead < n_sub and ahead % 16 == place and who(ahead) == "P":
+                        pass_through(ahead)
                 regroup(s)
                 while next_load < len(loads) and max(load_users[next_load - NB]) <= s:
                     load_piece(next_load)

@@ -14,13 +14,13 @@ ADD = mybir.AluOpType.add
 FLOPS = 2 * 256 * 2048 * 6144
 
 P = 128
-NB = 6
+NB = 12
 GB = 8
 CB = 16
 TB = 4
 SB = 6
 LQ = 1
-LEAD = {3: 4, 6: 5, 12: 6}
+LEAD = {3: 4, 6: 5, 10: 6}
 HYBRID = (False, False, True)
 N_G = 6
 
@@ -29,10 +29,8 @@ def who(s):
     third, i = divmod(s, 16)
     if third == 0:
         return "VS"[i % 2]
-    if i in (3, 6, 12):
+    if i in (3, 6, 10):
         return "P"
-    if third == 1:
-        return "V" if i == 0 or i >= 11 and i % 2 == 1 else "S"
     return "V" if i >= 9 and i % 2 == 1 else "S"
 
 
@@ -85,7 +83,7 @@ def tile_attention_pa_kernel(tc, x, rope, qkv_w, out_0, out_1, out_2):
         loads = []
         for ch in chunk_seq:
             g, c = divmod(ch, 4)
-            width = 2 if ch < 5 else 4
+            width = 2
             for first in range(0, 4, width):
                 loads.append((g, c, first, width))
         load_users = [[s for s, (g, c, nb) in enumerate(order) if (g, c) == (lg, lc) and first <= nb < first + width]

@@ -20,7 +20,7 @@ CB = 16
 TB = 4
 SB = 6
 LQ = 1
-LEAD = {3: 4, 6: 5, 10: 6}
+LEAD = {3: 3, 6: 5, 10: 6}
 HYBRID = (False, False, True)
 N_G = 6
 

from contextlib import ExitStack

import concourse.mybir as mybir
from concourse.masks import make_identity

F32 = mybir.dt.float32
BF16 = mybir.dt.bfloat16
U32 = mybir.dt.uint32
U8 = mybir.dt.uint8
FP8X4 = mybir.dt.float8_e4m3fn_x4
MULT = mybir.AluOpType.mult
ADD = mybir.AluOpType.add

FLOPS = 2 * 256 * 2048 * 6144

P = 128
NB = 12
GB = 8
CB = 16
TB = 4
SB = 6
LQ = 1
LEAD = {3: 3, 6: 5, 10: 6}
HYBRID = (False, False, True)
N_G = 6


def who(s):
    third, i = divmod(s, 16)
    if third == 0:
        return "VS"[i % 2]
    if i in (3, 6, 10):
        return "P"
    return "V" if i >= 9 and i % 2 == 1 else "S"


def sub_block_order():
    order = []
    for g in range(3):
        if HYBRID[g]:
            for c in range(2):
                for nb in range(4):
                    order.append((g, c, nb))
            for nb in range(4):
                for c in range(2, 4):
                    order.append((g, c, nb))
        else:
            for c in range(4):
                for nb in range(4):
                    order.append((g, c, nb))
    return order


def tile_attention_pa_kernel(tc, x, rope, qkv_w, out_0, out_1, out_2):
    nc = tc.nc
    outs = (out_0, out_1, out_2)
    order = sub_block_order()
    n_sub = len(order)
    last_of = {}
    for s, (g, c, nb) in enumerate(order):
        last_of[(g, nb)] = s
    users = {}
    chunk_seq = []
    for s, (g, c, nb) in enumerate(order):
        ch = 4 * g + c
        if ch not in users:
            users[ch] = []
            chunk_seq.append(ch)
        users[ch].append(s)

    with ExitStack() as ctx:
        const = ctx.enter_context(tc.tile_pool(name="const", bufs=1))
        rawp = ctx.enter_context(tc.tile_pool(name="rawp", bufs=NB))
        grp = ctx.enter_context(tc.tile_pool(name="grp", bufs=GB))
        cod = ctx.enter_context(tc.tile_pool(name="cod", bufs=CB))
        tmp = ctx.enter_context(tc.tile_pool(name="tmp", bufs=TB))
        stg = ctx.enter_context(tc.tile_pool(name="stg", bufs=SB))
        psum = ctx.enter_context(tc.psum_pool(name="psum", bufs=1))

        ctx.enter_context(tc.manual_schedule(engines={mybir.EngineType.PE}))
        raw = {}

        loads = []
        for ch in chunk_seq:
            g, c = divmod(ch, 4)
            width = 2
            for first in range(0, 4, width):
                loads.append((g, c, first, width))
        load_users = [[s for s, (g, c, nb) in enumerate(order) if (g, c) == (lg, lc) and first <= nb < first + width]
                      for lg, lc, first, width in loads]

        def load_piece(k):
            g, c, first, width = loads[k]
            t = rawp.tile([P, 4, 512 * width], BF16, name="raw%d" % k, tag="raw")
            lo = 2048 * g + 512 * first
            nc.sync.dma_start(out=t[:], in_=qkv_w[512 * c:512 * (c + 1), lo:lo + 512 * width].rearrange("(p t) w -> p t w", t=4))
            for i in range(width):
                raw[(g, c, first + i)] = t[:, :, 512 * i:512 * (i + 1)]

        x_sb = const.tile([P, 4096], BF16, name="x_sb")
        rp = const.tile([P, 2, 64, 2], BF16, name="rp")
        for k in range(NB):
            load_piece(k)
            if k == 3:
                for b in range(2):
                    nc.sync.dma_start(out=x_sb[b:P:2, :], in_=x[b].rearrange("(i e) k -> i (e k)", e=2))
            if k == 4:
                for b in range(2):
                    nc.sync.dma_start(out=rp[b:P:2].rearrange("p e j r -> p (e j r)"),
                                      in_=rope.rearrange("(i e) o d -> i (e o d)", e=2))
        next_load = NB

        ident = const.tile([P, P], F32, name="ident")
        make_identity(nc, ident[:])
        ident16 = const.tile([P, P], BF16, name="ident16")
        make_identity(nc, ident16[:])
        tbl = const.tile([P, 2, 2, 64, 2], F32, name="tbl")
        nc.gpsimd.tensor_copy(out=tbl[:, :, 0, :, :], in_=rp[:])
        nc.gpsimd.tensor_scalar(out=tbl[:, :, 1, :, 0], in0=rp[:, :, :, 1], scalar1=-1.0, scalar2=0.0, op0=MULT, op1=ADD)
        nc.gpsimd.tensor_copy(out=tbl[:, :, 1, :, 1], in_=rp[:, :, :, 0])

        xw = x_sb[:].bitcast(F32)
        gx = const.tile([P, 4096], BF16, name="gx", align_bytes=64)
        gxf = gx[:].bitcast(F32)
        xc = const.tile([P, 1024], U32, name="xc", align_bytes=64)
        xs = const.tile([P, 1024], U8, name="xs", align_bytes=64)
        xt = []
        for c in range(4):
            t = psum.tile([P, 2, 2, P], F32, name="xt%d" % c, tag="bank%d" % (2 * c))
            xt.append(t)
            for e in range(2):
                for u in range(2):
                    lo = 1024 * e + 256 * c + u
                    nc.tensor.transpose(t[:, e, u, :], xw[:, lo:lo + 255:2], ident[:])

        def x_path():
            for c in range(4):
                dst = gxf[:, 512 * c:512 * (c + 1)].rearrange("p (e r u) -> p e r u", e=2, u=2)
                srcv = xt[c][:].rearrange("p e u r -> p e r u")
                if c % 2 == 0:
                    nc.vector.tensor_copy(out=dst, in_=srcv)
                else:
                    nc.scalar.copy(out=dst, in_=srcv)
            for c in range(4):
                nc.vector.quantize_mx(out=xc[:, 256 * c:256 * (c + 1)].bitcast(FP8X4),
                                      scales=xs[:, 256 * c:256 * (c + 1)],
                                      in_=gx[:, 1024 * c:1024 * (c + 1)])

        grouped = {}
        codes = {}
        acc = {}
        passed = {}

        def pass_through(s):
            g, c, nb = order[s]
            passed[s] = []
            for h in range(2):
                t = psum.tile([P, 256, 4], BF16, name="pass%d_%d" % (s, h), tag="bank%d" % (6 + h))
                passed[s].append(t)
                lo = 256 * h
                for j in range(2):
                    nc.tensor.matmul(t[:].rearrange("p n t -> p t n")[:, 2 * j:2 * j + 2, :], lhsT=ident16[:],
                                     rhs=raw[(g, c, nb)][:, 2 * j:2 * j + 2, lo:lo + 256], start=True, stop=True)

        def regroup(s):
            g, c, nb = order[s]
            t = grp.tile([P, 512, 4], BF16, name="grouped%d" % s, tag="grouped", align_bytes=64)
            grouped[s] = t
            if who(s) == "P":
                flat = t[:].rearrange("p w t -> p (w t)").bitcast(F32)
                for h in range(2):
                    nc.scalar.copy(out=flat[:, 512 * h:512 * (h + 1)],
                                   in_=passed[s][h][:].rearrange("p n t -> p (n t)").bitcast(F32))
                return
            srcv = raw[(g, c, nb)].rearrange("p t (c i) -> p c t i", i=8)
            dst = t[:].rearrange("p (c i) t -> p c t i", i=8)
            if who(s) == "V":
                nc.vector.tensor_copy(out=dst, in_=srcv)
            else:
                nc.scalar.copy(out=dst, in_=srcv)

        def quantise(s):
            w = cod.tile([P, 512], U32, name="words%d" % s, tag="words", align_bytes=64)
            sc = cod.tile([P, 512], U8, name="scales%d" % s, tag="scales", align_bytes=64)
            codes[s] = (w, sc)
            nc.vector.quantize_mx(out=w[:].bitcast(FP8X4), scales=sc[:],
                                  in_=grouped[s][:].rearrange("p w t -> p (w t)"))

        def multiply(s):
            g, c, nb = order[s]
            w, sc = codes[s]
            for e in range(2):
                if c == 0:
                    acc[(g, nb, e)] = psum.tile([P, 512], F32, name="acc%d_%d_%d" % (g, nb, e), tag="bank%d" % (2 * ((4 * g + nb) % 3) + e))
                lo = 256 * c + 128 * e
                nc.tensor.matmul_mx(out=acc[(g, nb, e)][:],
                                    lhsT=xc[:, lo:lo + 128].bitcast(FP8X4), lhsT_scale=xs[:, lo:lo + 128],
                                    rhs=w[:].bitcast(FP8X4), rhs_scale=sc[:],
                                    start=(c == 0), stop=(c == 3))

        def store(g, nb, stage):
            for b in range(2):
                nc.sync.dma_start(out=outs[g][b, 4 * nb:4 * nb + 4].rearrange("h (i e) d -> i h (e d)", e=2),
                                  in_=stage[b:P:2].rearrange("p h e d -> p h (e d)"))

        def products(g, nb, e):
            pr = tmp.tile([P, 2, 4, 64, 2], F32, name="prod%d_%d_%d" % (g, nb, e), tag="prod")
            in0 = acc[(g, nb, e)][:].rearrange("p (h j r) -> p r h j", h=4, r=2).unsqueeze(4).to_broadcast([P, 2, 4, 64, 2])
            in1 = tbl[:, e].unsqueeze(2).to_broadcast([P, 2, 4, 64, 2])
            nc.vector.tensor_tensor(out=pr[:], in0=in0, in1=in1, op=MULT)
            return pr

        def add_products(engine, stage, e, pr):
            engine.tensor_tensor(out=stage[:, :, e, :], in0=pr[:, 0].rearrange("p h j r -> p h (j r)"),
                                 in1=pr[:, 1].rearrange("p h j r -> p h (j r)"), op=ADD)

        def rope_burst(g):
            late = []
            n = 0
            for nb in range(4):
                stage = stg.tile([P, 4, 2, P], F32, name="stage%d_%d" % (g, nb), tag="stage")
                for e in range(2):
                    pr = products(g, nb, e)
                    if n < N_G:
                        add_products(nc.gpsimd, stage, e, pr)
                    else:
                        late.append((nb, stage, e, pr))
                    n += 1
                if n <= N_G:
                    store(g, nb, stage)
                if nb == 0:
                    release_held()
            for nb, stage, e, pr in late:
                add_products(nc.vector, stage, e, pr)
                if e == 1:
                    store(g, nb, stage)

        def copy_out(g, nb):
            stage = stg.tile([P, 4, 2, P], F32, name="stage%d_%d" % (g, nb), tag="stage")
            for e in range(2):
                srcv = acc[(g, nb, e)][:].rearrange("p (h d) -> p h d", h=4)
                if nb == 3 and e == 0:
                    nc.vector.tensor_copy(out=stage[:, :, e, :], in_=srcv)
                else:
                    nc.scalar.copy(out=stage[:, :, e, :], in_=srcv)
            store(g, nb, stage)

        held = []

        def release_held():
            for k in held:
                multiply(k)
            held.clear()

        x_path()
        for s in range(n_sub + LQ):
            if s < n_sub:
                for place in LEAD:
                    ahead = s + LEAD[place]
                    if ahead < n_sub and ahead % 16 == place and who(ahead) == "P":
                        pass_through(ahead)
                regroup(s)
                while next_load < len(loads) and max(load_users[next_load - NB]) <= s:
                    load_piece(next_load)
                    next_load += 1
            m = s - LQ
            if m >= 0:
                quantise(m)
                g, c, nb = order[m]
                if nb == 3 and (g < 2 or c < 2):
                    held.append(m)
                else:
                    multiply(m)
                if g < 2 and m == 16 * g + 15:
                    rope_burst(g)
                if g == 2 and last_of[(g, nb)] == m:
                    copy_out(g, nb)
                    if nb == 0:
                        release_held()
